import numpy as np
import ml_dtypes


BF16 = ml_dtypes.bfloat16


def bf(x):
    return np.asarray(x, np.float32).astype(BF16)


def f64(x):
    return np.asarray(x).astype(np.float64)


E2M1 = np.array([0.0, 0.5, 1.0, 1.5, 2.0, 3.0, 4.0, 6.0, -0.0, -0.5, -1.0, -1.5, -2.0, -3.0, -4.0, -6.0])


def pack_weight(w, fmt):
    k, n = w.shape
    w = f64(bf(w)).reshape(k // 32, 32, n)
    amax = np.abs(w).max(1)
    if fmt == "e4m3":
        byte = np.frexp(amax)[1] - 1 + 127 - 7
    else:
        mant, ex = np.frexp(amax / 6.0)
        byte = np.where(mant > 0.5, ex, ex - 1) + 127
    byte = np.clip(np.where(amax > 0, byte, 1), 1, 254)
    scaled = (w * np.exp2(127.0 - byte)[:, None, :]).reshape(k, n).astype(np.float32)
    by_word = np.ascontiguousarray(scaled.reshape(k // 512, 128, 4, n).transpose(0, 1, 3, 2))
    if fmt == "e4m3":
        words = by_word.astype(ml_dtypes.float8_e4m3fn).view(np.uint8)
    else:
        c = by_word.astype(ml_dtypes.float4_e2m1fn).view(np.uint8) & 0xF
        words = c[..., 0::2] | (c[..., 1::2] << 4)
    return np.ascontiguousarray(words), np.ascontiguousarray(byte.astype(np.uint8).reshape(k // 512, 16, n))


def unpack_weight(words, scales, fmt):
    g, p, n, _ = words.shape
    if fmt == "e4m3":
        vals = np.ascontiguousarray(words).view(ml_dtypes.float8_e4m3fn).astype(np.float64)
    else:
        nib = np.empty((g, p, n, 4), np.uint8)
        nib[..., 0::2] = words & 0xF
        nib[..., 1::2] = words >> 4
        vals = E2M1[nib]
    vals = vals * np.repeat(np.exp2(scales.astype(np.float64) - 127.0), 8, axis=1)[..., None]
    return vals.transpose(0, 1, 3, 2).reshape(g * 512, n)

def pack4(w):
    words, scales = pack_weight(w, "e2m1")
    return words.reshape(words.shape[0], 128, -1), scales


def unpack4(words, scales):
    return unpack_weight(words.reshape(words.shape[0], 128, -1, 2), scales, "e2m1")


def kspread(k):
    return np.exp2(np.repeat(np.random.randint(-6, 7, k // 32), 32).astype(np.float64))


S, B, H, NH, HD = 512, 1, 1536, 16, 128
ROTARY_BASE = 10000.0
ROT = HD // 4


def rotate_half(x):
    x1, x2 = np.split(x, 2, axis=3)
    return np.concatenate((-x2, x1), axis=3)


def rope_cos_sin():
    inv_freq = ROTARY_BASE ** (-(np.arange(0, ROT, 2, dtype=np.float64) / ROT))
    t = np.arange(S, dtype=np.float64)
    freqs = t[:, None] * inv_freq[None, :]
    emb = np.concatenate((freqs, freqs), axis=freqs.ndim - freqs.ndim // 2)
    return np.cos(emb)[:, None, None, :], np.sin(emb)[:, None, None, :]


def setup_inputs():
    s = kspread(H)
    hidden_states = np.random.standard_normal((S, B, H)) * s
    hidden_states_words, hidden_states_scales = pack4(np.ascontiguousarray(hidden_states.reshape(S * B, H).T))
    words, scales = pack4(np.random.standard_normal((H, NH * 3 * HD)) / np.sqrt(H) / s[:, None])
    b_qkv = bf(np.random.standard_normal(NH * 3 * HD) * 0.3)
    return {"hidden_states_words": hidden_states_words,
            "hidden_states_scales": hidden_states_scales,
            "W_qkv_words": words,
            "W_qkv_scales": scales,
            "b_qkv": b_qkv}


def reference(hidden_states_words, hidden_states_scales, W_qkv_words, W_qkv_scales, b_qkv):
    mixed = ((unpack4(hidden_states_words, hidden_states_scales).T.reshape(S, B, H) @ unpack4(W_qkv_words, W_qkv_scales)) + f64(b_qkv)).reshape(S, B, NH, 3 * HD)
    q, k, v = np.split(mixed, 3, axis=3)
    q_rot, q_pass = q[..., :ROT], q[..., ROT:]
    k_rot, k_pass = k[..., :ROT], k[..., ROT:]
    cos, sin = rope_cos_sin()
    q_rot = q_rot * cos + rotate_half(q_rot) * sin
    k_rot = k_rot * cos + rotate_half(k_rot) * sin
    q = np.concatenate((q_rot, q_pass), axis=3)
    k = np.concatenate((k_rot, k_pass), axis=3)
    return q, k, v

@@ -1,0 +1,334 @@
+import math
+from contextlib import ExitStack
+
+import concourse.mybir as mybir
+
+F32 = mybir.dt.float32
+BF16 = mybir.dt.bfloat16
+I32 = mybir.dt.int32
+U8 = mybir.dt.uint8
+FP4X4 = mybir.dt.float4_e2m1fn_x4
+ALU = mybir.AluOpType
+ACT = mybir.ActivationFunctionType
+
+P = 128
+TOKENS = 512
+HIDDEN = 1536
+HEADS = 16
+HEAD_DIM = 128
+HEAD_COLS = 3 * HEAD_DIM
+COLS = HEADS * HEAD_COLS
+PASSES = HIDDEN // 512
+TOK_TILES = TOKENS // P
+BANK = 512
+HALF = 16
+
+FLOPS = 2 * TOKENS * HIDDEN * COLS
+
+TWO_PI = 2.0 * math.pi
+C1 = round(TWO_PI * 2.0 ** 14) / 2.0 ** 14
+C2 = round((TWO_PI - C1) * 2.0 ** 31) / 2.0 ** 31
+C3 = TWO_PI - C1 - C2
+
+GROUPS = ((0, 4), (4, 4), (8, 8))
+CODE_CHUNKS = ((512, 1536), (1536, 3072), (3072, 4608), (4608, 6144))
+PLANE_CHUNKS = ((0, 1536), (1536, 6144))
+N_WARM = 8
+
+
+def tile_gptneoxattention_pa_kernel(
+    tc, hid_words, hid_scales, w_words, w_scales, b_qkv, out_q, out_k, out_v
+):
+    nc = tc.nc
+    outs = (out_q, out_k, out_v)
+
+    with ExitStack() as ctx:
+        const = ctx.enter_context(tc.tile_pool(name="const", bufs=1))
+        tmp_pool = ctx.enter_context(tc.tile_pool(name="tmp", bufs=3))
+        psum = ctx.enter_context(tc.psum_pool(name="psum", bufs=8))
+
+        hid_plane = const.tile([P, PASSES, TOKENS], U8, name="hid_plane", align_bytes=64)
+        w_planes = []
+        for i, (a, b) in enumerate(PLANE_CHUNKS):
+            wp = const.tile([P, PASSES, b - a], U8, name="w_plane%d" % i, align_bytes=64)
+            w_planes.append(wp)
+
+        def load_plane(plane, src):
+            for q in range(4):
+                nc.sync.dma_start(
+                    out=plane[32 * q : 32 * q + 4, :, :].bitcast(I32),
+                    in_=src[:, 4 * q : 4 * q + 4, :].rearrange("g r n -> r g n").bitcast(I32),
+                )
+
+        hid_first = const.tile([P, 2 * TOKENS], U8, name="hid_first", align_bytes=64)
+        hid_rest = const.tile([P, PASSES - 1, 2 * TOKENS], U8, name="hid_rest", align_bytes=64)
+        w_first = const.tile([P, 2 * BANK], U8, name="w_first", align_bytes=64)
+        w_first_rest = const.tile([P, PASSES - 1, 2 * BANK], U8, name="w_first_rest", align_bytes=64)
+        nc.sync.dma_start(out=hid_first[:].bitcast(I32), in_=hid_words[0].bitcast(I32))
+        nc.sync.dma_start(out=w_first[:].bitcast(I32), in_=w_words[0, :, 0 : 2 * BANK].bitcast(I32))
+        nc.vector.memset(w_planes[0][:].bitcast(I32), 0)
+        nc.vector.memset(hid_plane[:].bitcast(I32), 0)
+        load_plane(w_planes[0], w_scales[:, :, 0:1536])
+        load_plane(hid_plane, hid_scales)
+
+        zeros = const.tile([P, BANK], BF16, name="zeros")
+        nc.gpsimd.memset(zeros[:].bitcast(F32), 0.0)
+        warm_acc = psum.tile([P, BANK], F32, name="acc", tag="acc")
+        for i in range(N_WARM):
+            nc.tensor.matmul(out=warm_acc[:], lhsT=zeros[:, 0:P], rhs=zeros[:], start=True, stop=True)
+
+        bias = const.tile([P, COLS], BF16, name="bias")
+        nc.gpsimd.dma_start(out=bias[:, 0:1536], in_=b_qkv[0:1536].partition_broadcast(P))
+
+        nc.sync.dma_start(
+            out=hid_rest[:].bitcast(I32),
+            in_=hid_words[1:PASSES].rearrange("g p n -> p g n").bitcast(I32),
+        )
+        nc.sync.dma_start(
+            out=w_first_rest[:].bitcast(I32),
+            in_=w_words[1:PASSES, :, 0 : 2 * BANK].rearrange("g p n -> p g n").bitcast(I32),
+        )
+
+        nc.vector.memset(w_planes[1][:].bitcast(I32), 0)
+        w_chunks = []
+
+        def load_codes(i):
+            a, b = CODE_CHUNKS[i]
+            wc = const.tile([P, PASSES, 2 * (b - a)], U8, name="w_codes%d" % i, align_bytes=64)
+            nc.sync.dma_start(
+                out=wc[:].bitcast(I32),
+                in_=w_words[:, :, 2 * a : 2 * b].rearrange("g p n -> p g n").bitcast(I32),
+            )
+            w_chunks.append(wc)
+
+        load_codes(0)
+        nc.sync.dma_start(out=bias[:, 1536:COLS], in_=b_qkv[1536:COLS].partition_broadcast(P))
+        load_plane(w_planes[1], w_scales[:, :, 1536:6144])
+        load_codes(1)
+        load_codes(2)
+        load_codes(3)
+
+        warm = const.tile([P, 1], F32, name="warm")
+        nc.gpsimd.memset(warm[:], 0.0)
+        nc.scalar.activation(out=warm[:], in_=warm[:], func=ACT.Sin)
+
+        pos = const.tile([P, TOK_TILES], F32, name="pos")
+        nc.gpsimd.iota(
+            pos[:], pattern=[[P, TOK_TILES]], base=0, channel_multiplier=1,
+            allow_small_or_imprecise_dtypes=True,
+        )
+        table_shape = [P, TOK_TILES, HALF]
+        ang = const.tile(table_shape, F32, name="ang")
+        nc.vector.tensor_copy(out=ang[:, :, 0:1], in_=pos[:].unsqueeze(2))
+        for w in (1, 2, 4, 8):
+            nc.vector.tensor_scalar(
+                out=ang[:, :, w : 2 * w], in0=ang[:, :, 0:w],
+                scalar1=10000.0 ** (-w / 16.0), scalar2=None, op0=ALU.mult,
+            )
+        turns_i = const.tile(table_shape, I32, name="turns_i")
+        nc.vector.tensor_scalar(
+            out=turns_i[:], in0=ang[:], scalar1=1.0 / TWO_PI, scalar2=0.25,
+            op0=ALU.mult, op1=ALU.add,
+        )
+        turns = const.tile(table_shape, F32, name="turns")
+        nc.vector.tensor_copy(out=turns[:], in_=turns_i[:])
+        red = const.tile(table_shape, F32, name="red")
+        nc.vector.scalar_tensor_tensor(
+            out=red[:], in0=turns[:], scalar=-C1, in1=ang[:], op0=ALU.mult, op1=ALU.add
+        )
+        for cc in (C2, C3):
+            nc.vector.scalar_tensor_tensor(
+                out=red[:], in0=turns[:], scalar=-cc, in1=red[:], op0=ALU.mult, op1=ALU.add
+            )
+        sin_half = const.tile(table_shape, F32, name="sin_half")
+        sin_quarter = const.tile(table_shape, F32, name="sin_quarter")
+        nc.scalar.activation(out=sin_half[:], in_=red[:], func=ACT.Sin, scale=0.5)
+        nc.scalar.activation(out=sin_quarter[:], in_=red[:], func=ACT.Sin, scale=0.25)
+        cos_t = const.tile(table_shape, F32, name="cos_t")
+        sin_t = const.tile(table_shape, F32, name="sin_t")
+        cos_half = const.tile(table_shape, F32, name="cos_half")
+        nc.vector.tensor_tensor(out=cos_t[:], in0=sin_half[:], in1=sin_half[:], op=ALU.mult)
+        nc.vector.tensor_scalar(
+            out=cos_t[:], in0=cos_t[:], scalar1=-2.0, scalar2=1.0, op0=ALU.mult, op1=ALU.add
+        )
+        nc.vector.tensor_tensor(out=cos_half[:], in0=sin_quarter[:], in1=sin_quarter[:], op=ALU.mult)
+        nc.vector.tensor_scalar(
+            out=cos_half[:], in0=cos_half[:], scalar1=-2.0, scalar2=1.0, op0=ALU.mult, op1=ALU.add
+        )
+        nc.vector.scalar_tensor_tensor(
+            out=sin_t[:], in0=sin_half[:], scalar=2.0, in1=cos_half[:], op0=ALU.mult, op1=ALU.mult
+        )
+
+        def w_operand(col, n, g):
+            if col < BANK:
+                if g == 0:
+                    codes = w_first[:, 2 * col : 2 * (col + n)]
+                else:
+                    codes = w_first_rest[:, g - 1, 2 * col : 2 * (col + n)]
+            else:
+                i = [k for k, (a, b) in enumerate(CODE_CHUNKS) if a <= col < b][0]
+                off = col - CODE_CHUNKS[i][0]
+                codes = w_chunks[i][:, g, 2 * off : 2 * (off + n)]
+            i = [k for k, (a, b) in enumerate(PLANE_CHUNKS) if a <= col < b][0]
+            off = col - PLANE_CHUNKS[i][0]
+            return codes.bitcast(FP4X4), w_planes[i][:, g, off : off + n]
+
+        def one_pass(out, col, n, m, g):
+            codes, plane = w_operand(col, n, g)
+            if g == 0:
+                tokens = hid_first[:, 2 * P * m : 2 * P * (m + 1)]
+            else:
+                tokens = hid_rest[:, g - 1, 2 * P * m : 2 * P * (m + 1)]
+            nc.tensor.matmul_mx(
+                out=out,
+                lhsT=tokens.bitcast(FP4X4),
+                lhsT_scale=hid_plane[:, g, P * m : P * (m + 1)],
+                rhs=codes,
+                rhs_scale=plane,
+                start=(g == 0),
+                stop=(g == PASSES - 1),
+            )
+
+        stages = {}
+        for gi, (h0, nh) in enumerate(GROUPS):
+            for m in range(TOK_TILES):
+                st = const.tile([P, 3, nh, HEAD_DIM], F32, name="stage_%d_%d" % (gi, m))
+                stages[(gi, m)] = st
+
+        def group_of(head):
+            return [gi for gi, (h0, nh) in enumerate(GROUPS) if h0 <= head < h0 + nh][0]
+
+        bias_heads = bias[:].rearrange("p (h k d) -> p h k d", k=3, d=HEAD_DIM)
+
+        def evacuate(acc, c, m):
+            blocks = [divmod(4 * c + i, 3) for i in range(4)]
+            start = 0
+            for i in range(1, 5):
+                if i == 4 or blocks[i][0] != blocks[start][0]:
+                    head, kind = blocks[start]
+                    n = i - start
+                    gi = group_of(head)
+                    nc.vector.tensor_tensor(
+                        out=stages[(gi, m)][:, kind : kind + n, head - GROUPS[gi][0], :],
+                        in0=acc[:, P * start : P * i].rearrange("p (b d) -> p b d", d=HEAD_DIM),
+                        in1=bias_heads[:, head, kind : kind + n, :],
+                        op=ALU.add,
+                    )
+                    start = i
+
+        def bank_job(c, m):
+            acc = psum.tile([P, BANK], F32, name="acc", tag="acc")
+            for g in range(PASSES):
+                one_pass(acc[:], c * BANK, BANK, m, g)
+            evacuate(acc, c, m)
+
+        def qk_bank_job(head, m):
+            acc = psum.tile([P, BANK], F32, name="acc", tag="acc")
+            for i in range(2):
+                for g in range(PASSES):
+                    one_pass(acc[:, 256 * i : 256 * (i + 1)], (head + i) * HEAD_COLS, 256, m, g)
+            gi = group_of(head)
+            hl = head - GROUPS[gi][0]
+            nc.vector.tensor_tensor(
+                out=stages[(gi, m)][:, 0:2, hl : hl + 2, :].rearrange("p k h d -> p h k d"),
+                in0=acc[:].rearrange("p (h k d) -> p h k d", k=2, d=HEAD_DIM),
+                in1=bias_heads[:, head : head + 2, 0:2, :],
+                op=ALU.add,
+            )
+
+        def v_bank_job(head, m):
+            acc = psum.tile([P, BANK], F32, name="acc", tag="acc")
+            for i in range(4):
+                for g in range(PASSES):
+                    one_pass(
+                        acc[:, P * i : P * (i + 1)], (head + i) * HEAD_COLS + 2 * HEAD_DIM, P, m, g
+                    )
+            gi = group_of(head)
+            hl = head - GROUPS[gi][0]
+            nc.vector.tensor_tensor(
+                out=stages[(gi, m)][:, 2, hl : hl + 4, :],
+                in0=acc[:].rearrange("p (h d) -> p h d", d=HEAD_DIM),
+                in1=bias_heads[:, head : head + 4, 2, :],
+                op=ALU.add,
+            )
+
+        def store(gi, m, kind, hl=0, n=None):
+            h0, nh = GROUPS[gi]
+            n = nh if n is None else n
+            nc.sync.dma_start(
+                out=outs[kind][P * m : P * (m + 1), 0, h0 + hl : h0 + hl + n, :],
+                in_=stages[(gi, m)][:, kind, hl : hl + n, :],
+            )
+
+        def rope_products(gi, m):
+            st = stages[(gi, m)]
+            nh = GROUPS[gi][1]
+            by_cos = tmp_pool.tile([P, HALF, 2, nh, 2], F32, name="by_cos", tag="by_cos%d" % nh)
+            by_sin = tmp_pool.tile([P, HALF, 2, nh, 2], F32, name="by_sin", tag="by_sin%d" % nh)
+            for j in range(HALF):
+                src = st[:, 0:2, :, j : j + HALF + 1 : HALF]
+                nc.scalar.activation(
+                    out=by_cos[:, j, :, :, :], in_=src, func=ACT.Copy, scale=cos_t[:, m, j : j + 1]
+                )
+                nc.scalar.activation(
+                    out=by_sin[:, j, :, :, :], in_=src, func=ACT.Copy, scale=sin_t[:, m, j : j + 1]
+                )
+            return by_cos, by_sin
+
+        def rope_sums(gi, m, engine, by_cos, by_sin):
+            st = stages[(gi, m)]
+            engine.tensor_tensor(
+                out=st[:, 0:2, :, 0:HALF],
+                in0=by_cos[:, :, :, :, 0].rearrange("p j k h -> p k h j"),
+                in1=by_sin[:, :, :, :, 1].rearrange("p j k h -> p k h j"),
+                op=ALU.subtract,
+            )
+            engine.tensor_tensor(
+                out=st[:, 0:2, :, HALF : 2 * HALF],
+                in0=by_cos[:, :, :, :, 1].rearrange("p j k h -> p k h j"),
+                in1=by_sin[:, :, :, :, 0].rearrange("p j k h -> p k h j"),
+                op=ALU.add,
+            )
+
+        def finish(gi, m):
+            store(gi, m, 2)
+            by_cos, by_sin = rope_products(gi, m)
+            rope_sums(gi, m, nc.gpsimd, by_cos, by_sin)
+            store(gi, m, 0)
+            store(gi, m, 1)
+
+        accs = []
+        for m in range(TOK_TILES):
+            acc = psum.tile([P, BANK], F32, name="acc", tag="acc")
+            accs.append(acc)
+        for g in range(PASSES):
+            for m in range(TOK_TILES):
+                one_pass(accs[m][:], 0, BANK, m, g)
+        for m in range(TOK_TILES):
+            evacuate(accs[m], 0, m)
+
+        for m in range(TOK_TILES):
+            bank_job(1, m)
+            bank_job(2, m)
+            finish(0, m)
+        for m in range(TOK_TILES):
+            for c in range(3, 6):
+                bank_job(c, m)
+            finish(1, m)
+
+        for m in range(TOK_TILES):
+            for head in (8, 10, 12, 14):
+                qk_bank_job(head, m)
+            by_cos, by_sin = rope_products(2, m)
+            if m < TOK_TILES - 1:
+                rope_sums(2, m, nc.gpsimd, by_cos, by_sin)
+                store(2, m, 0)
+                store(2, m, 1)
+        for m in range(TOK_TILES):
+            if m == 2:
+                rope_sums(2, 3, nc.vector, by_cos, by_sin)
+                store(2, 3, 0)
+                store(2, 3, 1)
+            for head in (8, 12):
+                v_bank_job(head, m)
+                store(2, m, 2, head - 8, 4)

@@ -2,6 +2,7 @@ import math
 from contextlib import ExitStack
 
 import concourse.mybir as mybir
+from concourse.masks import make_identity
 
 F32 = mybir.dt.float32
 BF16 = mybir.dt.bfloat16
@@ -22,6 +23,8 @@ PASSES = HIDDEN // 512
 TOK_TILES = TOKENS // P
 BANK = 512
 HALF = 16
+BIAS_ROWS = 4
+BIAS_ROW = COLS // BIAS_ROWS
 
 FLOPS = 2 * TOKENS * HIDDEN * COLS
 
@@ -30,10 +33,10 @@ C1 = round(TWO_PI * 2.0 ** 14) / 2.0 ** 14
 C2 = round((TWO_PI - C1) * 2.0 ** 31) / 2.0 ** 31
 C3 = TWO_PI - C1 - C2
 
-GROUPS = ((0, 4), (4, 4), (8, 8))
-CODE_CHUNKS = ((512, 1536), (1536, 3072), (3072, 4608), (4608, 6144))
-PLANE_CHUNKS = ((0, 1536), (1536, 6144))
-N_WARM = 8
+GROUPS = ((0, 8), (8, 8))
+CODE_CHUNKS = ((512, 1536), (1536, 3072), (3072, 6144))
+PLANE_CHUNKS = ((0, 1536), (1536, 3072), (3072, 6144))
+N_WARM = 6
 
 
 def tile_gptneoxattention_pa_kernel(
@@ -43,6 +46,7 @@ def tile_gptneoxattention_pa_kernel(
     outs = (out_q, out_k, out_v)
 
     with ExitStack() as ctx:
+        ctx.enter_context(tc.manual_schedule(engines={mybir.EngineType.SP}))
         const = ctx.enter_context(tc.tile_pool(name="const", bufs=1))
         tmp_pool = ctx.enter_context(tc.tile_pool(name="tmp", bufs=3))
         psum = ctx.enter_context(tc.psum_pool(name="psum", bufs=8))
@@ -52,34 +56,43 @@ def tile_gptneoxattention_pa_kernel(
         for i, (a, b) in enumerate(PLANE_CHUNKS):
             wp = const.tile([P, PASSES, b - a], U8, name="w_plane%d" % i, align_bytes=64)
             w_planes.append(wp)
-
-        def load_plane(plane, src):
-            for q in range(4):
-                nc.sync.dma_start(
-                    out=plane[32 * q : 32 * q + 4, :, :].bitcast(I32),
-                    in_=src[:, 4 * q : 4 * q + 4, :].rearrange("g r n -> r g n").bitcast(I32),
-                )
-
         hid_first = const.tile([P, 2 * TOKENS], U8, name="hid_first", align_bytes=64)
         hid_rest = const.tile([P, PASSES - 1, 2 * TOKENS], U8, name="hid_rest", align_bytes=64)
         w_first = const.tile([P, 2 * BANK], U8, name="w_first", align_bytes=64)
         w_first_rest = const.tile([P, PASSES - 1, 2 * BANK], U8, name="w_first_rest", align_bytes=64)
-        nc.sync.dma_start(out=hid_first[:].bitcast(I32), in_=hid_words[0].bitcast(I32))
-        nc.sync.dma_start(out=w_first[:].bitcast(I32), in_=w_words[0, :, 0 : 2 * BANK].bitcast(I32))
+        w_chunks = []
+        for i, (a, b) in enumerate(CODE_CHUNKS):
+            wc = const.tile([P, PASSES, 2 * (b - a)], U8, name="w_codes%d" % i, align_bytes=64)
+            w_chunks.append(wc)
+        bias_rows = const.tile([P, BIAS_ROW], BF16, name="bias_rows")
+
+        def load_plane(plane, src):
+            for r in range(4):
+                nc.sync.dma_start(
+                    out=plane[r : P : 32, :, :].bitcast(I32),
+                    in_=src[:, r : 16 : 4, :].rearrange("g q n -> q g n").bitcast(I32),
+                )
+
+        def load_codes(i):
+            a, b = CODE_CHUNKS[i]
+            nc.sync.dma_start(
+                out=w_chunks[i][:].bitcast(I32),
+                in_=w_words[:, :, 2 * a : 2 * b].rearrange("g p n -> p g n").bitcast(I32),
+            )
+
+        nc.vector.memset(bias_rows[:], 0.0)
         nc.vector.memset(w_planes[0][:].bitcast(I32), 0)
         nc.vector.memset(hid_plane[:].bitcast(I32), 0)
+        nc.vector.memset(w_planes[1][:].bitcast(I32), 0)
+        nc.vector.memset(w_planes[2][:].bitcast(I32), 0)
+
+        nc.sync.dma_start(out=hid_first[:].bitcast(I32), in_=hid_words[0].bitcast(I32))
+        nc.sync.dma_start(out=w_first[:].bitcast(I32), in_=w_words[0, :, 0 : 2 * BANK].bitcast(I32))
+        nc.sync.dma_start(
+            out=bias_rows[0:BIAS_ROWS, :], in_=b_qkv.rearrange("(r n) -> r n", r=BIAS_ROWS)
+        )
         load_plane(w_planes[0], w_scales[:, :, 0:1536])
         load_plane(hid_plane, hid_scales)
-
-        zeros = const.tile([P, BANK], BF16, name="zeros")
-        nc.gpsimd.memset(zeros[:].bitcast(F32), 0.0)
-        warm_acc = psum.tile([P, BANK], F32, name="acc", tag="acc")
-        for i in range(N_WARM):
-            nc.tensor.matmul(out=warm_acc[:], lhsT=zeros[:, 0:P], rhs=zeros[:], start=True, stop=True)
-
-        bias = const.tile([P, COLS], BF16, name="bias")
-        nc.gpsimd.dma_start(out=bias[:, 0:1536], in_=b_qkv[0:1536].partition_broadcast(P))
-
         nc.sync.dma_start(
             out=hid_rest[:].bitcast(I32),
             in_=hid_words[1:PASSES].rearrange("g p n -> p g n").bitcast(I32),
@@ -88,25 +101,30 @@ def tile_gptneoxattention_pa_kernel(
             out=w_first_rest[:].bitcast(I32),
             in_=w_words[1:PASSES, :, 0 : 2 * BANK].rearrange("g p n -> p g n").bitcast(I32),
         )
-
-        nc.vector.memset(w_planes[1][:].bitcast(I32), 0)
-        w_chunks = []
-
-        def load_codes(i):
-            a, b = CODE_CHUNKS[i]
-            wc = const.tile([P, PASSES, 2 * (b - a)], U8, name="w_codes%d" % i, align_bytes=64)
-            nc.sync.dma_start(
-                out=wc[:].bitcast(I32),
-                in_=w_words[:, :, 2 * a : 2 * b].rearrange("g p n -> p g n").bitcast(I32),
-            )
-            w_chunks.append(wc)
-
         load_codes(0)
-        nc.sync.dma_start(out=bias[:, 1536:COLS], in_=b_qkv[1536:COLS].partition_broadcast(P))
-        load_plane(w_planes[1], w_scales[:, :, 1536:6144])
+        load_plane(w_planes[1], w_scales[:, :, 1536:3072])
         load_codes(1)
+        load_plane(w_planes[2], w_scales[:, :, 3072:6144])
         load_codes(2)
-        load_codes(3)
+
+        zeros = const.tile([P, BANK], BF16, name="zeros")
+        nc.gpsimd.memset(zeros[:].bitcast(F32), 0.0)
+        warm_acc = psum.tile([P, BANK], F32, name="acc", tag="acc")
+        for i in range(N_WARM):
+            nc.tensor.matmul(out=warm_acc[:], lhsT=zeros[:, 0:P], rhs=zeros[:], start=True, stop=True)
+
+        ident = const.tile([P, P], BF16, name="ident")
+        make_identity(nc, ident[:])
+        bias = const.tile([P, COLS], BF16, name="bias")
+
+        def spread_bias(c):
+            r, j = divmod(c * BANK, BIAS_ROW)
+            acc = psum.tile([P, BANK], F32, name="acc", tag="acc")
+            nc.tensor.matmul(
+                out=acc[:], lhsT=ident[:, r : r + 1].to_broadcast([P, P]),
+                rhs=bias_rows[:, j : j + BANK], start=True, stop=True,
+            )
+            nc.scalar.copy(out=bias[:, c * BANK : (c + 1) * BANK], in_=acc[:])
 
         warm = const.tile([P, 1], F32, name="warm")
         nc.gpsimd.memset(warm[:], 0.0)
@@ -290,12 +308,16 @@ def tile_gptneoxattention_pa_kernel(
                 op=ALU.add,
             )
 
-        def finish(gi, m):
-            store(gi, m, 2)
-            by_cos, by_sin = rope_products(gi, m)
-            rope_sums(gi, m, nc.gpsimd, by_cos, by_sin)
-            store(gi, m, 0)
-            store(gi, m, 1)
+        waiting = []
+
+        def flush_waiting():
+            for gi, m in waiting:
+                store(gi, m, 0)
+                store(gi, m, 1)
+            waiting.clear()
+
+        for c in range(6):
+            spread_bias(c)
 
         accs = []
         for m in range(TOK_TILES):
@@ -307,28 +329,36 @@ def tile_gptneoxattention_pa_kernel(
         for m in range(TOK_TILES):
             evacuate(accs[m], 0, m)
 
-        for m in range(TOK_TILES):
-            bank_job(1, m)
-            bank_job(2, m)
-            finish(0, m)
-        for m in range(TOK_TILES):
-            for c in range(3, 6):
+        for c in (1, 2):
+            for m in range(TOK_TILES):
                 bank_job(c, m)
-            finish(1, m)
+            for cb in range(3 * c + 3, 3 * c + 6):
+                spread_bias(cb)
+
+        for m in range(TOK_TILES):
+            for c in (3, 4, 5):
+                bank_job(c, m)
+            store(0, m, 2)
+            flush_waiting()
+            by_cos, by_sin = rope_products(0, m)
+            rope_sums(0, m, nc.gpsimd, by_cos, by_sin)
+            waiting.append((0, m))
 
         for m in range(TOK_TILES):
             for head in (8, 10, 12, 14):
                 qk_bank_job(head, m)
-            by_cos, by_sin = rope_products(2, m)
+            flush_waiting()
+            by_cos, by_sin = rope_products(1, m)
             if m < TOK_TILES - 1:
-                rope_sums(2, m, nc.gpsimd, by_cos, by_sin)
-                store(2, m, 0)
-                store(2, m, 1)
+                rope_sums(1, m, nc.gpsimd, by_cos, by_sin)
+                waiting.append((1, m))
         for m in range(TOK_TILES):
+            if m == 1:
+                flush_waiting()
             if m == 2:
-                rope_sums(2, 3, nc.vector, by_cos, by_sin)
-                store(2, 3, 0)
-                store(2, 3, 1)
+                rope_sums(1, 3, nc.vector, by_cos, by_sin)
+                store(1, 3, 0)
+                store(1, 3, 1)
             for head in (8, 12):
                 v_bank_job(head, m)
-                store(2, m, 2, head - 8, 4)
+                store(1, m, 2, head - 8, 4)

@@ -23,7 +23,7 @@ PASSES = HIDDEN // 512
 TOK_TILES = TOKENS // P
 BANK = 512
 HALF = 16
-BIAS_ROWS = 4
+BIAS_ROWS = 16
 BIAS_ROW = COLS // BIAS_ROWS
 
 FLOPS = 2 * TOKENS * HIDDEN * COLS
@@ -34,9 +34,9 @@ C2 = round((TWO_PI - C1) * 2.0 ** 31) / 2.0 ** 31
 C3 = TWO_PI - C1 - C2
 
 GROUPS = ((0, 8), (8, 8))
-CODE_CHUNKS = ((512, 1536), (1536, 3072), (3072, 6144))
-PLANE_CHUNKS = ((0, 1536), (1536, 3072), (3072, 6144))
-N_WARM = 6
+CODE_CHUNKS = ((512, 1024), (1024, 3072), (3072, 6144))
+PLANE_CHUNKS = ((0, 1024), (1024, 3072), (3072, 6144))
+N_WARM = 4
 
 
 def tile_gptneoxattention_pa_kernel(
@@ -46,7 +46,7 @@ def tile_gptneoxattention_pa_kernel(
     outs = (out_q, out_k, out_v)
 
     with ExitStack() as ctx:
-        ctx.enter_context(tc.manual_schedule(engines={mybir.EngineType.SP}))
+        ctx.enter_context(tc.manual_schedule())
         const = ctx.enter_context(tc.tile_pool(name="const", bufs=1))
         tmp_pool = ctx.enter_context(tc.tile_pool(name="tmp", bufs=3))
         psum = ctx.enter_context(tc.psum_pool(name="psum", bufs=8))
@@ -80,19 +80,18 @@ def tile_gptneoxattention_pa_kernel(
                 in_=w_words[:, :, 2 * a : 2 * b].rearrange("g p n -> p g n").bitcast(I32),
             )
 
-        nc.vector.memset(bias_rows[:], 0.0)
-        nc.vector.memset(w_planes[0][:].bitcast(I32), 0)
+        nc.vector.memset(bias_rows[:].bitcast(I32), 0)
         nc.vector.memset(hid_plane[:].bitcast(I32), 0)
+        nc.vector.memset(w_planes[0][:].bitcast(I32), 0)
         nc.vector.memset(w_planes[1][:].bitcast(I32), 0)
-        nc.vector.memset(w_planes[2][:].bitcast(I32), 0)
 
-        nc.sync.dma_start(out=hid_first[:].bitcast(I32), in_=hid_words[0].bitcast(I32))
-        nc.sync.dma_start(out=w_first[:].bitcast(I32), in_=w_words[0, :, 0 : 2 * BANK].bitcast(I32))
         nc.sync.dma_start(
             out=bias_rows[0:BIAS_ROWS, :], in_=b_qkv.rearrange("(r n) -> r n", r=BIAS_ROWS)
         )
-        load_plane(w_planes[0], w_scales[:, :, 0:1536])
+        nc.sync.dma_start(out=hid_first[:].bitcast(I32), in_=hid_words[0].bitcast(I32))
+        nc.sync.dma_start(out=w_first[:].bitcast(I32), in_=w_words[0, :, 0 : 2 * BANK].bitcast(I32))
         load_plane(hid_plane, hid_scales)
+        load_plane(w_planes[0], w_scales[:, :, 0:1024])
         nc.sync.dma_start(
             out=hid_rest[:].bitcast(I32),
             in_=hid_words[1:PASSES].rearrange("g p n -> p g n").bitcast(I32),
@@ -102,34 +101,16 @@ def tile_gptneoxattention_pa_kernel(
             in_=w_words[1:PASSES, :, 0 : 2 * BANK].rearrange("g p n -> p g n").bitcast(I32),
         )
         load_codes(0)
-        load_plane(w_planes[1], w_scales[:, :, 1536:3072])
+        load_plane(w_planes[1], w_scales[:, :, 1024:3072])
         load_codes(1)
-        load_plane(w_planes[2], w_scales[:, :, 3072:6144])
         load_codes(2)
 
         zeros = const.tile([P, BANK], BF16, name="zeros")
         nc.gpsimd.memset(zeros[:].bitcast(F32), 0.0)
-        warm_acc = psum.tile([P, BANK], F32, name="acc", tag="acc")
-        for i in range(N_WARM):
-            nc.tensor.matmul(out=warm_acc[:], lhsT=zeros[:, 0:P], rhs=zeros[:], start=True, stop=True)
-
-        ident = const.tile([P, P], BF16, name="ident")
-        make_identity(nc, ident[:])
-        bias = const.tile([P, COLS], BF16, name="bias")
-
-        def spread_bias(c):
-            r, j = divmod(c * BANK, BIAS_ROW)
-            acc = psum.tile([P, BANK], F32, name="acc", tag="acc")
-            nc.tensor.matmul(
-                out=acc[:], lhsT=ident[:, r : r + 1].to_broadcast([P, P]),
-                rhs=bias_rows[:, j : j + BANK], start=True, stop=True,
-            )
-            nc.scalar.copy(out=bias[:, c * BANK : (c + 1) * BANK], in_=acc[:])
-
         warm = const.tile([P, 1], F32, name="warm")
         nc.gpsimd.memset(warm[:], 0.0)
-        nc.scalar.activation(out=warm[:], in_=warm[:], func=ACT.Sin)
-
+        ident = const.tile([P, P], BF16, name="ident")
+        make_identity(nc, ident[:])
         pos = const.tile([P, TOK_TILES], F32, name="pos")
         nc.gpsimd.iota(
             pos[:], pattern=[[P, TOK_TILES]], base=0, channel_multiplier=1,
@@ -137,17 +118,26 @@ def tile_gptneoxattention_pa_kernel(
         )
         table_shape = [P, TOK_TILES, HALF]
         ang = const.tile(table_shape, F32, name="ang")
-        nc.vector.tensor_copy(out=ang[:, :, 0:1], in_=pos[:].unsqueeze(2))
+        nc.gpsimd.tensor_copy(out=ang[:, :, 0:1], in_=pos[:].unsqueeze(2))
         for w in (1, 2, 4, 8):
-            nc.vector.tensor_scalar(
+            nc.gpsimd.tensor_scalar(
                 out=ang[:, :, w : 2 * w], in0=ang[:, :, 0:w],
                 scalar1=10000.0 ** (-w / 16.0), scalar2=None, op0=ALU.mult,
             )
         turns_i = const.tile(table_shape, I32, name="turns_i")
-        nc.vector.tensor_scalar(
+        nc.gpsimd.tensor_scalar(
             out=turns_i[:], in0=ang[:], scalar1=1.0 / TWO_PI, scalar2=0.25,
             op0=ALU.mult, op1=ALU.add,
         )
+        nc.gpsimd.memset(w_planes[2][:].bitcast(F32), 0.0)
+        load_plane(w_planes[2], w_scales[:, :, 3072:6144])
+
+        nc.scalar.activation(out=warm[:], in_=warm[:], func=ACT.Sin)
+
+        warm_acc = psum.tile([P, BANK], F32, name="acc", tag="acc")
+        for i in range(N_WARM):
+            nc.tensor.matmul(out=warm_acc[:], lhsT=zeros[:, 0:P], rhs=zeros[:], start=True, stop=True)
+
         turns = const.tile(table_shape, F32, name="turns")
         nc.vector.tensor_copy(out=turns[:], in_=turns_i[:])
         red = const.tile(table_shape, F32, name="red")
@@ -160,22 +150,38 @@ def tile_gptneoxattention_pa_kernel(
             )
         sin_half = const.tile(table_shape, F32, name="sin_half")
         sin_quarter = const.tile(table_shape, F32, name="sin_quarter")
-        nc.scalar.activation(out=sin_half[:], in_=red[:], func=ACT.Sin, scale=0.5)
-        nc.scalar.activation(out=sin_quarter[:], in_=red[:], func=ACT.Sin, scale=0.25)
+
+        bias = const.tile([P, COLS], BF16, name="bias")
+        for j in range(BIAS_ROWS // 2):
+            acc = psum.tile([P, 2 * BANK], BF16, name="acc", tag="acc")
+            for i in range(2):
+                r = 2 * j + i
+                nc.tensor.matmul(
+                    out=acc[:, BIAS_ROW * i : BIAS_ROW * (i + 1)],
+                    lhsT=ident[:, r : r + 1].to_broadcast([P, P]),
+                    rhs=bias_rows[:], start=True, stop=True,
+                )
+            dst = bias[:, 2 * BIAS_ROW * j : 2 * BIAS_ROW * (j + 1)]
+            if j % 2 == 0:
+                nc.scalar.copy(out=dst, in_=acc[:, 0 : 2 * BIAS_ROW])
+            else:
+                nc.vector.tensor_copy(out=dst, in_=acc[:, 0 : 2 * BIAS_ROW])
+            if j == 0:
+                nc.scalar.activation(out=sin_half[:], in_=red[:], func=ACT.Sin, scale=0.5)
+                nc.scalar.activation(out=sin_quarter[:], in_=red[:], func=ACT.Sin, scale=0.25)
+
         cos_t = const.tile(table_shape, F32, name="cos_t")
         sin_t = const.tile(table_shape, F32, name="sin_t")
         cos_half = const.tile(table_shape, F32, name="cos_half")
-        nc.vector.tensor_tensor(out=cos_t[:], in0=sin_half[:], in1=sin_half[:], op=ALU.mult)
-        nc.vector.tensor_scalar(
+        nc.gpsimd.tensor_tensor(out=cos_t[:], in0=sin_half[:], in1=sin_half[:], op=ALU.mult)
+        nc.gpsimd.tensor_scalar(
             out=cos_t[:], in0=cos_t[:], scalar1=-2.0, scalar2=1.0, op0=ALU.mult, op1=ALU.add
         )
-        nc.vector.tensor_tensor(out=cos_half[:], in0=sin_quarter[:], in1=sin_quarter[:], op=ALU.mult)
-        nc.vector.tensor_scalar(
-            out=cos_half[:], in0=cos_half[:], scalar1=-2.0, scalar2=1.0, op0=ALU.mult, op1=ALU.add
+        nc.gpsimd.tensor_tensor(out=cos_half[:], in0=sin_quarter[:], in1=sin_quarter[:], op=ALU.mult)
+        nc.gpsimd.tensor_scalar(
+            out=cos_half[:], in0=cos_half[:], scalar1=-4.0, scalar2=2.0, op0=ALU.mult, op1=ALU.add
         )
-        nc.vector.scalar_tensor_tensor(
-            out=sin_t[:], in0=sin_half[:], scalar=2.0, in1=cos_half[:], op0=ALU.mult, op1=ALU.mult
-        )
+        nc.gpsimd.tensor_tensor(out=sin_t[:], in0=sin_half[:], in1=cos_half[:], op=ALU.mult)
 
         def w_operand(col, n, g):
             if col < BANK:
@@ -316,9 +322,6 @@ def tile_gptneoxattention_pa_kernel(
                 store(gi, m, 1)
             waiting.clear()
 
-        for c in range(6):
-            spread_bias(c)
-
         accs = []
         for m in range(TOK_TILES):
             acc = psum.tile([P, BANK], F32, name="acc", tag="acc")
@@ -332,8 +335,6 @@ def tile_gptneoxattention_pa_kernel(
         for c in (1, 2):
             for m in range(TOK_TILES):
                 bank_job(c, m)
-            for cb in range(3 * c + 3, 3 * c + 6):
-                spread_bias(cb)
 
         for m in range(TOK_TILES):
             for c in (3, 4, 5):

@@ -34,9 +34,9 @@ C2 = round((TWO_PI - C1) * 2.0 ** 31) / 2.0 ** 31
 C3 = TWO_PI - C1 - C2
 
 GROUPS = ((0, 8), (8, 8))
-CODE_CHUNKS = ((512, 1024), (1024, 3072), (3072, 6144))
-PLANE_CHUNKS = ((0, 1024), (1024, 3072), (3072, 6144))
-N_WARM = 4
+CODE_CHUNKS = ((512, 1536), (1536, 3072), (3072, 6144))
+PLANE_CHUNKS = ((0, 1536), (1536, 3072), (3072, 6144))
+N_WARM = 14
 
 
 def tile_gptneoxattention_pa_kernel(
@@ -80,6 +80,8 @@ def tile_gptneoxattention_pa_kernel(
                 in_=w_words[:, :, 2 * a : 2 * b].rearrange("g p n -> p g n").bitcast(I32),
             )
 
+        zeros = const.tile([P, P], BF16, name="zeros")
+        nc.vector.memset(zeros[:].bitcast(I32), 0)
         nc.vector.memset(bias_rows[:].bitcast(I32), 0)
         nc.vector.memset(hid_plane[:].bitcast(I32), 0)
         nc.vector.memset(w_planes[0][:].bitcast(I32), 0)
@@ -91,7 +93,7 @@ def tile_gptneoxattention_pa_kernel(
         nc.sync.dma_start(out=hid_first[:].bitcast(I32), in_=hid_words[0].bitcast(I32))
         nc.sync.dma_start(out=w_first[:].bitcast(I32), in_=w_words[0, :, 0 : 2 * BANK].bitcast(I32))
         load_plane(hid_plane, hid_scales)
-        load_plane(w_planes[0], w_scales[:, :, 0:1024])
+        load_plane(w_planes[0], w_scales[:, :, 0:1536])
         nc.sync.dma_start(
             out=hid_rest[:].bitcast(I32),
             in_=hid_words[1:PASSES].rearrange("g p n -> p g n").bitcast(I32),
@@ -101,14 +103,10 @@ def tile_gptneoxattention_pa_kernel(
             in_=w_words[1:PASSES, :, 0 : 2 * BANK].rearrange("g p n -> p g n").bitcast(I32),
         )
         load_codes(0)
-        load_plane(w_planes[1], w_scales[:, :, 1024:3072])
+        load_plane(w_planes[1], w_scales[:, :, 1536:3072])
         load_codes(1)
         load_codes(2)
 
-        zeros = const.tile([P, BANK], BF16, name="zeros")
-        nc.gpsimd.memset(zeros[:].bitcast(F32), 0.0)
-        warm = const.tile([P, 1], F32, name="warm")
-        nc.gpsimd.memset(warm[:], 0.0)
         ident = const.tile([P, P], BF16, name="ident")
         make_identity(nc, ident[:])
         pos = const.tile([P, TOK_TILES], F32, name="pos")
@@ -116,28 +114,41 @@ def tile_gptneoxattention_pa_kernel(
             pos[:], pattern=[[P, TOK_TILES]], base=0, channel_multiplier=1,
             allow_small_or_imprecise_dtypes=True,
         )
+
+        warm = const.tile([P, 1], F32, name="warm")
+        nc.scalar.activation(out=warm[:], in_=zeros[:, 0:1], func=ACT.Sin)
+
+        warm_acc = psum.tile([P, BANK], F32, name="acc", tag="acc")
+        for i in range(N_WARM):
+            nc.tensor.matmul(out=warm_acc[:, 0:P], lhsT=zeros[:], rhs=zeros[:], start=True, stop=True)
+
+        bias = const.tile([P, COLS], BF16, name="bias")
+        for j in range(BIAS_ROWS // 2):
+            acc = psum.tile([P, 2 * BANK], BF16, name="acc", tag="acc")
+            for i in range(2):
+                r = 2 * j + i
+                nc.tensor.matmul(
+                    out=acc[:, BIAS_ROW * i : BIAS_ROW * (i + 1)],
+                    lhsT=ident[:, r : r + 1].to_broadcast([P, P]),
+                    rhs=bias_rows[:], start=True, stop=True,
+                )
+            nc.scalar.copy(
+                out=bias[:, 2 * BIAS_ROW * j : 2 * BIAS_ROW * (j + 1)], in_=acc[:, 0 : 2 * BIAS_ROW]
+            )
+
         table_shape = [P, TOK_TILES, HALF]
         ang = const.tile(table_shape, F32, name="ang")
-        nc.gpsimd.tensor_copy(out=ang[:, :, 0:1], in_=pos[:].unsqueeze(2))
+        nc.vector.tensor_copy(out=ang[:, :, 0:1], in_=pos[:].unsqueeze(2))
         for w in (1, 2, 4, 8):
-            nc.gpsimd.tensor_scalar(
+            nc.vector.tensor_scalar(
                 out=ang[:, :, w : 2 * w], in0=ang[:, :, 0:w],
                 scalar1=10000.0 ** (-w / 16.0), scalar2=None, op0=ALU.mult,
             )
         turns_i = const.tile(table_shape, I32, name="turns_i")
-        nc.gpsimd.tensor_scalar(
+        nc.vector.tensor_scalar(
             out=turns_i[:], in0=ang[:], scalar1=1.0 / TWO_PI, scalar2=0.25,
             op0=ALU.mult, op1=ALU.add,
         )
-        nc.gpsimd.memset(w_planes[2][:].bitcast(F32), 0.0)
-        load_plane(w_planes[2], w_scales[:, :, 3072:6144])
-
-        nc.scalar.activation(out=warm[:], in_=warm[:], func=ACT.Sin)
-
-        warm_acc = psum.tile([P, BANK], F32, name="acc", tag="acc")
-        for i in range(N_WARM):
-            nc.tensor.matmul(out=warm_acc[:], lhsT=zeros[:, 0:P], rhs=zeros[:], start=True, stop=True)
-
         turns = const.tile(table_shape, F32, name="turns")
         nc.vector.tensor_copy(out=turns[:], in_=turns_i[:])
         red = const.tile(table_shape, F32, name="red")
@@ -150,38 +161,30 @@ def tile_gptneoxattention_pa_kernel(
             )
         sin_half = const.tile(table_shape, F32, name="sin_half")
         sin_quarter = const.tile(table_shape, F32, name="sin_quarter")
+        nc.scalar.activation(out=sin_half[:], in_=red[:], func=ACT.Sin, scale=0.5)
+        nc.scalar.activation(out=sin_quarter[:], in_=red[:], func=ACT.Sin, scale=0.25)
 
-        bias = const.tile([P, COLS], BF16, name="bias")
-        for j in range(BIAS_ROWS // 2):
-            acc = psum.tile([P, 2 * BANK], BF16, name="acc", tag="acc")
-            for i in range(2):
-                r = 2 * j + i
-                nc.tensor.matmul(
-                    out=acc[:, BIAS_ROW * i : BIAS_ROW * (i + 1)],
-                    lhsT=ident[:, r : r + 1].to_broadcast([P, P]),
-                    rhs=bias_rows[:], start=True, stop=True,
-                )
-            dst = bias[:, 2 * BIAS_ROW * j : 2 * BIAS_ROW * (j + 1)]
-            if j % 2 == 0:
-                nc.scalar.copy(out=dst, in_=acc[:, 0 : 2 * BIAS_ROW])
-            else:
-                nc.vector.tensor_copy(out=dst, in_=acc[:, 0 : 2 * BIAS_ROW])
-            if j == 0:
-                nc.scalar.activation(out=sin_half[:], in_=red[:], func=ACT.Sin, scale=0.5)
-                nc.scalar.activation(out=sin_quarter[:], in_=red[:], func=ACT.Sin, scale=0.25)
+        nc.vector.memset(w_planes[2][:].bitcast(I32), 0)
+        load_plane(w_planes[2], w_scales[:, :, 3072:6144])
 
         cos_t = const.tile(table_shape, F32, name="cos_t")
         sin_t = const.tile(table_shape, F32, name="sin_t")
         cos_half = const.tile(table_shape, F32, name="cos_half")
-        nc.gpsimd.tensor_tensor(out=cos_t[:], in0=sin_half[:], in1=sin_half[:], op=ALU.mult)
-        nc.gpsimd.tensor_scalar(
-            out=cos_t[:], in0=cos_t[:], scalar1=-2.0, scalar2=1.0, op0=ALU.mult, op1=ALU.add
-        )
-        nc.gpsimd.tensor_tensor(out=cos_half[:], in0=sin_quarter[:], in1=sin_quarter[:], op=ALU.mult)
-        nc.gpsimd.tensor_scalar(
-            out=cos_half[:], in0=cos_half[:], scalar1=-4.0, scalar2=2.0, op0=ALU.mult, op1=ALU.add
-        )
-        nc.gpsimd.tensor_tensor(out=sin_t[:], in0=sin_half[:], in1=cos_half[:], op=ALU.mult)
+
+        def finish_tables():
+            nc.vector.tensor_tensor(out=cos_t[:], in0=sin_half[:], in1=sin_half[:], op=ALU.mult)
+            nc.vector.tensor_scalar(
+                out=cos_t[:], in0=cos_t[:], scalar1=-2.0, scalar2=1.0, op0=ALU.mult, op1=ALU.add
+            )
+            nc.vector.tensor_tensor(
+                out=cos_half[:], in0=sin_quarter[:], in1=sin_quarter[:], op=ALU.mult
+            )
+            nc.vector.tensor_scalar(
+                out=cos_half[:], in0=cos_half[:], scalar1=-2.0, scalar2=1.0, op0=ALU.mult, op1=ALU.add
+            )
+            nc.vector.scalar_tensor_tensor(
+                out=sin_t[:], in0=sin_half[:], scalar=2.0, in1=cos_half[:], op0=ALU.mult, op1=ALU.mult
+            )
 
         def w_operand(col, n, g):
             if col < BANK:
@@ -331,6 +334,7 @@ def tile_gptneoxattention_pa_kernel(
                 one_pass(accs[m][:], 0, BANK, m, g)
         for m in range(TOK_TILES):
             evacuate(accs[m], 0, m)
+        finish_tables()
 
         for c in (1, 2):
             for m in range(TOK_TILES):

@@ -123,18 +123,26 @@ def tile_gptneoxattention_pa_kernel(
             nc.tensor.matmul(out=warm_acc[:, 0:P], lhsT=zeros[:], rhs=zeros[:], start=True, stop=True)
 
         bias = const.tile([P, COLS], BF16, name="bias")
-        for j in range(BIAS_ROWS // 2):
+        bias_heads = bias[:].rearrange("p (h k d) -> p h k d", k=3, d=HEAD_DIM)
+
+        def spread_bias(heads, k0, k1):
+            n = HEAD_DIM * (k1 - k0)
             acc = psum.tile([P, 2 * BANK], BF16, name="acc", tag="acc")
-            for i in range(2):
-                r = 2 * j + i
+            for i, r in enumerate(heads):
                 nc.tensor.matmul(
-                    out=acc[:, BIAS_ROW * i : BIAS_ROW * (i + 1)],
+                    out=acc[:, n * i : n * (i + 1)],
                     lhsT=ident[:, r : r + 1].to_broadcast([P, P]),
-                    rhs=bias_rows[:], start=True, stop=True,
+                    rhs=bias_rows[:, HEAD_DIM * k0 : HEAD_DIM * k1], start=True, stop=True,
                 )
             nc.scalar.copy(
-                out=bias[:, 2 * BIAS_ROW * j : 2 * BIAS_ROW * (j + 1)], in_=acc[:, 0 : 2 * BIAS_ROW]
+                out=bias_heads[:, heads[0] : heads[0] + len(heads), k0:k1, :],
+                in_=acc[:, 0 : n * len(heads)].rearrange("p (h k d) -> p h k d", k=k1 - k0, d=HEAD_DIM),
             )
+
+        for h in range(0, 8, 2):
+            spread_bias((h, h + 1), 0, 3)
+        for h in range(8, HEADS, 4):
+            spread_bias((h, h + 1, h + 2, h + 3), 0, 2)
 
         table_shape = [P, TOK_TILES, HALF]
         ang = const.tile(table_shape, F32, name="ang")
@@ -224,8 +232,6 @@ def tile_gptneoxattention_pa_kernel(
 
         def group_of(head):
             return [gi for gi, (h0, nh) in enumerate(GROUPS) if h0 <= head < h0 + nh][0]
-
-        bias_heads = bias[:].rearrange("p (h k d) -> p h k d", k=3, d=HEAD_DIM)
 
         def evacuate(acc, c, m):
             blocks = [divmod(4 * c + i, 3) for i in range(4)]
@@ -353,6 +359,8 @@ def tile_gptneoxattention_pa_kernel(
             for head in (8, 10, 12, 14):
                 qk_bank_job(head, m)
             flush_waiting()
+            if m == TOK_TILES - 1:
+                spread_bias((8, 9, 10, 11, 12, 13, 14, 15), 2, 3)
             by_cos, by_sin = rope_products(1, m)
             if m < TOK_TILES - 1:
                 rope_sums(1, m, nc.gpsimd, by_cos, by_sin)

@@ -37,6 +37,10 @@ GROUPS = ((0, 8), (8, 8))
 CODE_CHUNKS = ((512, 1536), (1536, 3072), (3072, 6144))
 PLANE_CHUNKS = ((0, 1536), (1536, 3072), (3072, 6144))
 N_WARM = 14
+LEAD_HID_CODES = 0
+LEAD_HID_PLANE = 64
+LEAD_W_CODES = 128
+LEAD_W_PLANE = 192
 
 
 def tile_gptneoxattention_pa_kernel(
@@ -51,19 +55,21 @@ def tile_gptneoxattention_pa_kernel(
         tmp_pool = ctx.enter_context(tc.tile_pool(name="tmp", bufs=3))
         psum = ctx.enter_context(tc.psum_pool(name="psum", bufs=8))
 
-        hid_plane = const.tile([P, PASSES, TOKENS], U8, name="hid_plane", align_bytes=64)
+        def operand_tile(name, passes, width, lead):
+            raw = const.tile([P, lead + passes * width], U8, name=name, align_bytes=256)
+            return raw[:, lead : lead + passes * width].rearrange("p (g n) -> p g n", g=passes)
+
+        hid_plane = operand_tile("hid_plane", PASSES, TOKENS, LEAD_HID_PLANE)
         w_planes = []
         for i, (a, b) in enumerate(PLANE_CHUNKS):
-            wp = const.tile([P, PASSES, b - a], U8, name="w_plane%d" % i, align_bytes=64)
-            w_planes.append(wp)
-        hid_first = const.tile([P, 2 * TOKENS], U8, name="hid_first", align_bytes=64)
-        hid_rest = const.tile([P, PASSES - 1, 2 * TOKENS], U8, name="hid_rest", align_bytes=64)
-        w_first = const.tile([P, 2 * BANK], U8, name="w_first", align_bytes=64)
-        w_first_rest = const.tile([P, PASSES - 1, 2 * BANK], U8, name="w_first_rest", align_bytes=64)
+            w_planes.append(operand_tile("w_plane%d" % i, PASSES, b - a, LEAD_W_PLANE))
+        hid_first = operand_tile("hid_first", 1, 2 * TOKENS, LEAD_HID_CODES)[:, 0, :]
+        hid_rest = operand_tile("hid_rest", PASSES - 1, 2 * TOKENS, LEAD_HID_CODES)
+        w_first = operand_tile("w_first", 1, 2 * BANK, LEAD_W_CODES)[:, 0, :]
+        w_first_rest = operand_tile("w_first_rest", PASSES - 1, 2 * BANK, LEAD_W_CODES)
         w_chunks = []
         for i, (a, b) in enumerate(CODE_CHUNKS):
-            wc = const.tile([P, PASSES, 2 * (b - a)], U8, name="w_codes%d" % i, align_bytes=64)
-            w_chunks.append(wc)
+            w_chunks.append(operand_tile("w_codes%d" % i, PASSES, 2 * (b - a), LEAD_W_CODES))
         bias_rows = const.tile([P, BIAS_ROW], BF16, name="bias_rows")
 
         def load_plane(plane, src):

@@ -178,7 +178,7 @@ def tile_gptneoxattention_pa_kernel(
         nc.scalar.activation(out=sin_half[:], in_=red[:], func=ACT.Sin, scale=0.5)
         nc.scalar.activation(out=sin_quarter[:], in_=red[:], func=ACT.Sin, scale=0.25)
 
-        nc.vector.memset(w_planes[2][:].bitcast(I32), 0)
+        nc.gpsimd.memset(w_planes[2][:].bitcast(F32), 0.0)
         load_plane(w_planes[2], w_scales[:, :, 3072:6144])
 
         cos_t = const.tile(table_shape, F32, name="cos_t")

@@ -233,7 +233,7 @@ def tile_gptneoxattention_pa_kernel(
         stages = {}
         for gi, (h0, nh) in enumerate(GROUPS):
             for m in range(TOK_TILES):
-                st = const.tile([P, 3, nh, HEAD_DIM], F32, name="stage_%d_%d" % (gi, m))
+                st = const.tile([P, 3, nh, HEAD_DIM], F32, name="stage_%d_%d" % (gi, m), align_bytes=256)
                 stages[(gi, m)] = st
 
         def group_of(head):

@@ -23,8 +23,7 @@ PASSES = HIDDEN // 512
 TOK_TILES = TOKENS // P
 BANK = 512
 HALF = 16
-BIAS_ROWS = 16
-BIAS_ROW = COLS // BIAS_ROWS
+WORD_COLS = COLS // 2 // P
 
 FLOPS = 2 * TOKENS * HIDDEN * COLS
 
@@ -70,7 +69,7 @@ def tile_gptneoxattention_pa_kernel(
         w_chunks = []
         for i, (a, b) in enumerate(CODE_CHUNKS):
             w_chunks.append(operand_tile("w_codes%d" % i, PASSES, 2 * (b - a), LEAD_W_CODES))
-        bias_rows = const.tile([P, BIAS_ROW], BF16, name="bias_rows")
+        bias_in = const.tile([P, 2 * WORD_COLS], BF16, name="bias_in")
 
         def load_plane(plane, src):
             for r in range(4):
@@ -88,14 +87,11 @@ def tile_gptneoxattention_pa_kernel(
 
         zeros = const.tile([P, P], BF16, name="zeros")
         nc.vector.memset(zeros[:].bitcast(I32), 0)
-        nc.vector.memset(bias_rows[:].bitcast(I32), 0)
         nc.vector.memset(hid_plane[:].bitcast(I32), 0)
         nc.vector.memset(w_planes[0][:].bitcast(I32), 0)
         nc.vector.memset(w_planes[1][:].bitcast(I32), 0)
 
-        nc.sync.dma_start(
-            out=bias_rows[0:BIAS_ROWS, :], in_=b_qkv.rearrange("(r n) -> r n", r=BIAS_ROWS)
-        )
+        nc.sync.dma_start(out=bias_in[:], in_=b_qkv.rearrange("(p c) -> p c", p=P))
         nc.sync.dma_start(out=hid_first[:].bitcast(I32), in_=hid_words[0].bitcast(I32))
         nc.sync.dma_start(out=w_first[:].bitcast(I32), in_=w_words[0, :, 0 : 2 * BANK].bitcast(I32))
         load_plane(hid_plane, hid_scales)
@@ -113,7 +109,7 @@ def tile_gptneoxattention_pa_kernel(
         load_codes(1)
         load_codes(2)
 
-        ident = const.tile([P, P], BF16, name="ident")
+        ident = const.tile([P, P], F32, name="ident")
         make_identity(nc, ident[:])
         pos = const.tile([P, TOK_TILES], F32, name="pos")
         nc.gpsimd.iota(
@@ -130,25 +126,19 @@ def tile_gptneoxattention_pa_kernel(
 
         bias = const.tile([P, COLS], BF16, name="bias")
         bias_heads = bias[:].rearrange("p (h k d) -> p h k d", k=3, d=HEAD_DIM)
-
-        def spread_bias(heads, k0, k1):
-            n = HEAD_DIM * (k1 - k0)
-            acc = psum.tile([P, 2 * BANK], BF16, name="acc", tag="acc")
-            for i, r in enumerate(heads):
-                nc.tensor.matmul(
-                    out=acc[:, n * i : n * (i + 1)],
-                    lhsT=ident[:, r : r + 1].to_broadcast([P, P]),
-                    rhs=bias_rows[:, HEAD_DIM * k0 : HEAD_DIM * k1], start=True, stop=True,
+        bias_words = bias[:].bitcast(F32).rearrange("p (n c) -> p n c", c=WORD_COLS)
+        bias_in_words = bias_in[:].bitcast(F32)
+        for c0 in range(0, WORD_COLS, 4):
+            acc = psum.tile([P, BANK], F32, name="acc", tag="acc")
+            for i in range(4):
+                nc.tensor.transpose(
+                    acc[:, P * i : P * (i + 1)],
+                    bias_in_words[:, c0 + i : c0 + i + 1].to_broadcast([P, P]),
+                    ident[:],
                 )
             nc.scalar.copy(
-                out=bias_heads[:, heads[0] : heads[0] + len(heads), k0:k1, :],
-                in_=acc[:, 0 : n * len(heads)].rearrange("p (h k d) -> p h k d", k=k1 - k0, d=HEAD_DIM),
+                out=bias_words[:, :, c0 : c0 + 4], in_=acc[:].rearrange("p (c n) -> p n c", c=4)
             )
-
-        for h in range(0, 8, 2):
-            spread_bias((h, h + 1), 0, 3)
-        for h in range(8, HEADS, 4):
-            spread_bias((h, h + 1, h + 2, h + 3), 0, 2)
 
         table_shape = [P, TOK_TILES, HALF]
         ang = const.tile(table_shape, F32, name="ang")
@@ -365,8 +355,6 @@ def tile_gptneoxattention_pa_kernel(
             for head in (8, 10, 12, 14):
                 qk_bank_job(head, m)
             flush_waiting()
-            if m == TOK_TILES - 1:
-                spread_bias((8, 9, 10, 11, 12, 13, 14, 15), 2, 3)
             by_cos, by_sin = rope_products(1, m)
             if m < TOK_TILES - 1:
                 rope_sums(1, m, nc.gpsimd, by_cos, by_sin)

@@ -37,9 +37,9 @@ CODE_CHUNKS = ((512, 1536), (1536, 3072), (3072, 6144))
 PLANE_CHUNKS = ((0, 1536), (1536, 3072), (3072, 6144))
 N_WARM = 14
 LEAD_HID_CODES = 0
-LEAD_HID_PLANE = 64
-LEAD_W_CODES = 128
-LEAD_W_PLANE = 192
+LEAD_HID_PLANE = 0
+LEAD_W_CODES = 0
+LEAD_W_PLANE = 0
 
 
 def tile_gptneoxattention_pa_kernel(

@@ -36,6 +36,7 @@ GROUPS = ((0, 8), (8, 8))
 CODE_CHUNKS = ((512, 1536), (1536, 3072), (3072, 6144))
 PLANE_CHUNKS = ((0, 1536), (1536, 3072), (3072, 6144))
 N_WARM = 14
+V_EARLY = 1
 LEAD_HID_CODES = 0
 LEAD_HID_PLANE = 0
 LEAD_W_CODES = 0
@@ -306,18 +307,19 @@ def tile_gptneoxattention_pa_kernel(
 
         def rope_sums(gi, m, engine, by_cos, by_sin):
             st = stages[(gi, m)]
-            engine.tensor_tensor(
-                out=st[:, 0:2, :, 0:HALF],
-                in0=by_cos[:, :, :, :, 0].rearrange("p j k h -> p k h j"),
-                in1=by_sin[:, :, :, :, 1].rearrange("p j k h -> p k h j"),
-                op=ALU.subtract,
-            )
-            engine.tensor_tensor(
-                out=st[:, 0:2, :, HALF : 2 * HALF],
-                in0=by_cos[:, :, :, :, 1].rearrange("p j k h -> p k h j"),
-                in1=by_sin[:, :, :, :, 0].rearrange("p j k h -> p k h j"),
-                op=ALU.add,
-            )
+            for kind in range(2):
+                engine.tensor_tensor(
+                    out=st[:, kind, :, 0:HALF],
+                    in0=by_cos[:, :, kind, :, 0].rearrange("p j h -> p h j"),
+                    in1=by_sin[:, :, kind, :, 1].rearrange("p j h -> p h j"),
+                    op=ALU.subtract,
+                )
+                engine.tensor_tensor(
+                    out=st[:, kind, :, HALF : 2 * HALF],
+                    in0=by_cos[:, :, kind, :, 1].rearrange("p j h -> p h j"),
+                    in1=by_sin[:, :, kind, :, 0].rearrange("p j h -> p h j"),
+                    op=ALU.add,
+                )
 
         waiting = []
 
@@ -338,12 +340,11 @@ def tile_gptneoxattention_pa_kernel(
             evacuate(accs[m], 0, m)
         finish_tables()
 
-        for c in (1, 2):
-            for m in range(TOK_TILES):
-                bank_job(c, m)
+        for m in range(TOK_TILES):
+            bank_job(1, m)
 
         for m in range(TOK_TILES):
-            for c in (3, 4, 5):
+            for c in (2, 3, 4, 5):
                 bank_job(c, m)
             store(0, m, 2)
             flush_waiting()
@@ -351,7 +352,15 @@ def tile_gptneoxattention_pa_kernel(
             rope_sums(0, m, nc.gpsimd, by_cos, by_sin)
             waiting.append((0, m))
 
+        def v_tile(m):
+            for head in (8, 12):
+                v_bank_job(head, m)
+                store(1, m, 2, head - 8, 4)
+
         for m in range(TOK_TILES):
+            if m == TOK_TILES - 1:
+                for early in range(V_EARLY):
+                    v_tile(early)
             for head in (8, 10, 12, 14):
                 qk_bank_job(head, m)
             flush_waiting()
@@ -359,13 +368,9 @@ def tile_gptneoxattention_pa_kernel(
             if m < TOK_TILES - 1:
                 rope_sums(1, m, nc.gpsimd, by_cos, by_sin)
                 waiting.append((1, m))
-        for m in range(TOK_TILES):
-            if m == 1:
-                flush_waiting()
-            if m == 2:
+        for m in range(V_EARLY, TOK_TILES):
+            if m == V_EARLY + 2:
                 rope_sums(1, 3, nc.vector, by_cos, by_sin)
                 store(1, 3, 0)
                 store(1, 3, 1)
-            for head in (8, 12):
-                v_bank_job(head, m)
-                store(1, m, 2, head - 8, 4)
+            v_tile(m)

@@ -23,6 +23,7 @@ PASSES = HIDDEN // 512
 TOK_TILES = TOKENS // P
 BANK = 512
 HALF = 16
+ROT = 2 * HALF
 WORD_COLS = COLS // 2 // P
 
 FLOPS = 2 * TOKENS * HIDDEN * COLS
@@ -37,6 +38,7 @@ CODE_CHUNKS = ((512, 1536), (1536, 3072), (3072, 6144))
 PLANE_CHUNKS = ((0, 1536), (1536, 3072), (3072, 6144))
 N_WARM = 14
 V_EARLY = 1
+SUMS_BEHIND = 3
 LEAD_HID_CODES = 0
 LEAD_HID_PLANE = 0
 LEAD_W_CODES = 0
@@ -227,6 +229,11 @@ def tile_gptneoxattention_pa_kernel(
                 st = const.tile([P, 3, nh, HEAD_DIM], F32, name="stage_%d_%d" % (gi, m), align_bytes=256)
                 stages[(gi, m)] = st
 
+        rotary = []
+        for m in range(TOK_TILES):
+            rot = const.tile([P, ROT, GROUPS[1][1], 2], F32, name="rotary_%d" % m)
+            rotary.append(rot)
+
         def group_of(head):
             return [gi for gi, (h0, nh) in enumerate(GROUPS) if h0 <= head < h0 + nh][0]
 
@@ -259,10 +266,17 @@ def tile_gptneoxattention_pa_kernel(
                     one_pass(acc[:, 256 * i : 256 * (i + 1)], (head + i) * HEAD_COLS, 256, m, g)
             gi = group_of(head)
             hl = head - GROUPS[gi][0]
+            sums = acc[:].rearrange("p (h k d) -> p h k d", k=2, d=HEAD_DIM)
             nc.vector.tensor_tensor(
-                out=stages[(gi, m)][:, 0:2, hl : hl + 2, :].rearrange("p k h d -> p h k d"),
-                in0=acc[:].rearrange("p (h k d) -> p h k d", k=2, d=HEAD_DIM),
-                in1=bias_heads[:, head : head + 2, 0:2, :],
+                out=stages[(gi, m)][:, 0:2, hl : hl + 2, ROT:HEAD_DIM].rearrange("p k h d -> p h k d"),
+                in0=sums[:, :, :, ROT:HEAD_DIM],
+                in1=bias_heads[:, head : head + 2, 0:2, ROT:HEAD_DIM],
+                op=ALU.add,
+            )
+            nc.vector.tensor_tensor(
+                out=rotary[m][:, :, hl : hl + 2, :],
+                in0=sums[:, :, :, 0:ROT].rearrange("p h k d -> p d h k"),
+                in1=bias_heads[:, head : head + 2, 0:2, 0:ROT].rearrange("p h k d -> p d h k"),
                 op=ALU.add,
             )
 
@@ -296,7 +310,7 @@ def tile_gptneoxattention_pa_kernel(
             by_cos = tmp_pool.tile([P, HALF, 2, nh, 2], F32, name="by_cos", tag="by_cos%d" % nh)
             by_sin = tmp_pool.tile([P, HALF, 2, nh, 2], F32, name="by_sin", tag="by_sin%d" % nh)
             for j in range(HALF):
-                src = st[:, 0:2, :, j : j + HALF + 1 : HALF]
+                src = st[:, 0:2, :, j : j + HALF + 1 : HALF] if gi == 0 else rotary[m][:, j : j + HALF + 1 : HALF, :, :]
                 nc.scalar.activation(
                     out=by_cos[:, j, :, :, :], in_=src, func=ACT.Copy, scale=cos_t[:, m, j : j + 1]
                 )
@@ -307,18 +321,19 @@ def tile_gptneoxattention_pa_kernel(
 
         def rope_sums(gi, m, engine, by_cos, by_sin):
             st = stages[(gi, m)]
+
+            def part(products, kind, t):
+                view = products[:, :, kind, :, t] if gi == 0 else products[:, :, t, :, kind]
+                return view.rearrange("p j h -> p h j")
+
             for kind in range(2):
                 engine.tensor_tensor(
                     out=st[:, kind, :, 0:HALF],
-                    in0=by_cos[:, :, kind, :, 0].rearrange("p j h -> p h j"),
-                    in1=by_sin[:, :, kind, :, 1].rearrange("p j h -> p h j"),
-                    op=ALU.subtract,
+                    in0=part(by_cos, kind, 0), in1=part(by_sin, kind, 1), op=ALU.subtract,
                 )
                 engine.tensor_tensor(
                     out=st[:, kind, :, HALF : 2 * HALF],
-                    in0=by_cos[:, :, kind, :, 1].rearrange("p j h -> p h j"),
-                    in1=by_sin[:, :, kind, :, 0].rearrange("p j h -> p h j"),
-                    op=ALU.add,
+                    in0=part(by_cos, kind, 1), in1=part(by_sin, kind, 0), op=ALU.add,
                 )
 
         waiting = []
@@ -368,9 +383,11 @@ def tile_gptneoxattention_pa_kernel(
             if m < TOK_TILES - 1:
                 rope_sums(1, m, nc.gpsimd, by_cos, by_sin)
                 waiting.append((1, m))
-        for m in range(V_EARLY, TOK_TILES):
-            if m == V_EARLY + 2:
+        late = [(m, head) for m in range(V_EARLY, TOK_TILES) for head in (8, 12)]
+        for i, (m, head) in enumerate(late):
+            if i == SUMS_BEHIND:
                 rope_sums(1, 3, nc.vector, by_cos, by_sin)
                 store(1, 3, 0)
                 store(1, 3, 1)
-            v_tile(m)
+            v_bank_job(head, m)
+            store(1, m, 2, head - 8, 4)

@@ -268,15 +268,15 @@ def tile_gptneoxattention_pa_kernel(
             hl = head - GROUPS[gi][0]
             sums = acc[:].rearrange("p (h k d) -> p h k d", k=2, d=HEAD_DIM)
             nc.vector.tensor_tensor(
-                out=stages[(gi, m)][:, 0:2, hl : hl + 2, ROT:HEAD_DIM].rearrange("p k h d -> p h k d"),
-                in0=sums[:, :, :, ROT:HEAD_DIM],
-                in1=bias_heads[:, head : head + 2, 0:2, ROT:HEAD_DIM],
-                op=ALU.add,
-            )
-            nc.vector.tensor_tensor(
                 out=rotary[m][:, :, hl : hl + 2, :],
                 in0=sums[:, :, :, 0:ROT].rearrange("p h k d -> p d h k"),
                 in1=bias_heads[:, head : head + 2, 0:2, 0:ROT].rearrange("p h k d -> p d h k"),
+                op=ALU.add,
+            )
+            nc.vector.tensor_tensor(
+                out=stages[(gi, m)][:, 0:2, hl : hl + 2, ROT:HEAD_DIM].rearrange("p k h d -> p h k d"),
+                in0=sums[:, :, :, ROT:HEAD_DIM],
+                in1=bias_heads[:, head : head + 2, 0:2, ROT:HEAD_DIM],
                 op=ALU.add,
             )
 

import math
from contextlib import ExitStack

import concourse.mybir as mybir
from concourse.masks import make_identity

F32 = mybir.dt.float32
BF16 = mybir.dt.bfloat16
I32 = mybir.dt.int32
U8 = mybir.dt.uint8
FP4X4 = mybir.dt.float4_e2m1fn_x4
ALU = mybir.AluOpType
ACT = mybir.ActivationFunctionType

P = 128
TOKENS = 512
HIDDEN = 1536
HEADS = 16
HEAD_DIM = 128
HEAD_COLS = 3 * HEAD_DIM
COLS = HEADS * HEAD_COLS
PASSES = HIDDEN // 512
TOK_TILES = TOKENS // P
BANK = 512
HALF = 16
ROT = 2 * HALF
WORD_COLS = COLS // 2 // P

FLOPS = 2 * TOKENS * HIDDEN * COLS

TWO_PI = 2.0 * math.pi
C1 = round(TWO_PI * 2.0 ** 14) / 2.0 ** 14
C2 = round((TWO_PI - C1) * 2.0 ** 31) / 2.0 ** 31
C3 = TWO_PI - C1 - C2

GROUPS = ((0, 8), (8, 8))
CODE_CHUNKS = ((512, 1536), (1536, 3072), (3072, 6144))
PLANE_CHUNKS = ((0, 1536), (1536, 3072), (3072, 6144))
N_WARM = 14
V_EARLY = 1
SUMS_BEHIND = 3
LEAD_HID_CODES = 0
LEAD_HID_PLANE = 0
LEAD_W_CODES = 0
LEAD_W_PLANE = 0


def tile_gptneoxattention_pa_kernel(
    tc, hid_words, hid_scales, w_words, w_scales, b_qkv, out_q, out_k, out_v
):
    nc = tc.nc
    outs = (out_q, out_k, out_v)

    with ExitStack() as ctx:
        ctx.enter_context(tc.manual_schedule())
        const = ctx.enter_context(tc.tile_pool(name="const", bufs=1))
        tmp_pool = ctx.enter_context(tc.tile_pool(name="tmp", bufs=3))
        psum = ctx.enter_context(tc.psum_pool(name="psum", bufs=8))

        def operand_tile(name, passes, width, lead):
            raw = const.tile([P, lead + passes * width], U8, name=name, align_bytes=256)
            return raw[:, lead : lead + passes * width].rearrange("p (g n) -> p g n", g=passes)

        hid_plane = operand_tile("hid_plane", PASSES, TOKENS, LEAD_HID_PLANE)
        w_planes = []
        for i, (a, b) in enumerate(PLANE_CHUNKS):
            w_planes.append(operand_tile("w_plane%d" % i, PASSES, b - a, LEAD_W_PLANE))
        hid_first = operand_tile("hid_first", 1, 2 * TOKENS, LEAD_HID_CODES)[:, 0, :]
        hid_rest = operand_tile("hid_rest", PASSES - 1, 2 * TOKENS, LEAD_HID_CODES)
        w_first = operand_tile("w_first", 1, 2 * BANK, LEAD_W_CODES)[:, 0, :]
        w_first_rest = operand_tile("w_first_rest", PASSES - 1, 2 * BANK, LEAD_W_CODES)
        w_chunks = []
        for i, (a, b) in enumerate(CODE_CHUNKS):
            w_chunks.append(operand_tile("w_codes%d" % i, PASSES, 2 * (b - a), LEAD_W_CODES))
        bias_in = const.tile([P, 2 * WORD_COLS], BF16, name="bias_in")

        def load_plane(plane, src):
            for r in range(4):
                nc.sync.dma_start(
                    out=plane[r : P : 32, :, :].bitcast(I32),
                    in_=src[:, r : 16 : 4, :].rearrange("g q n -> q g n").bitcast(I32),
                )

        def load_codes(i):
            a, b = CODE_CHUNKS[i]
            nc.sync.dma_start(
                out=w_chunks[i][:].bitcast(I32),
                in_=w_words[:, :, 2 * a : 2 * b].rearrange("g p n -> p g n").bitcast(I32),
            )

        zeros = const.tile([P, P], BF16, name="zeros")
        nc.vector.memset(zeros[:].bitcast(I32), 0)
        nc.vector.memset(hid_plane[:].bitcast(I32), 0)
        nc.vector.memset(w_planes[0][:].bitcast(I32), 0)
        nc.vector.memset(w_planes[1][:].bitcast(I32), 0)

        nc.sync.dma_start(out=bias_in[:], in_=b_qkv.rearrange("(p c) -> p c", p=P))
        nc.sync.dma_start(out=hid_first[:].bitcast(I32), in_=hid_words[0].bitcast(I32))
        nc.sync.dma_start(out=w_first[:].bitcast(I32), in_=w_words[0, :, 0 : 2 * BANK].bitcast(I32))
        load_plane(hid_plane, hid_scales)
        load_plane(w_planes[0], w_scales[:, :, 0:1536])
        nc.sync.dma_start(
            out=hid_rest[:].bitcast(I32),
            in_=hid_words[1:PASSES].rearrange("g p n -> p g n").bitcast(I32),
        )
        nc.sync.dma_start(
            out=w_first_rest[:].bitcast(I32),
            in_=w_words[1:PASSES, :, 0 : 2 * BANK].rearrange("g p n -> p g n").bitcast(I32),
        )
        load_codes(0)
        load_plane(w_planes[1], w_scales[:, :, 1536:3072])
        load_codes(1)
        load_codes(2)

        ident = const.tile([P, P], F32, name="ident")
        make_identity(nc, ident[:])
        pos = const.tile([P, TOK_TILES], F32, name="pos")
        nc.gpsimd.iota(
            pos[:], pattern=[[P, TOK_TILES]], base=0, channel_multiplier=1,
            allow_small_or_imprecise_dtypes=True,
        )

        warm = const.tile([P, 1], F32, name="warm")
        nc.scalar.activation(out=warm[:], in_=zeros[:, 0:1], func=ACT.Sin)

        warm_acc = psum.tile([P, BANK], F32, name="acc", tag="acc")
        for i in range(N_WARM):
            nc.tensor.matmul(out=warm_acc[:, 0:P], lhsT=zeros[:], rhs=zeros[:], start=True, stop=True)

        bias = const.tile([P, COLS], BF16, name="bias")
        bias_heads = bias[:].rearrange("p (h k d) -> p h k d", k=3, d=HEAD_DIM)
        bias_words = bias[:].bitcast(F32).rearrange("p (n c) -> p n c", c=WORD_COLS)
        bias_in_words = bias_in[:].bitcast(F32)
        for c0 in range(0, WORD_COLS, 4):
            acc = psum.tile([P, BANK], F32, name="acc", tag="acc")
            for i in range(4):
                nc.tensor.transpose(
                    acc[:, P * i : P * (i + 1)],
                    bias_in_words[:, c0 + i : c0 + i + 1].to_broadcast([P, P]),
                    ident[:],
                )
            nc.scalar.copy(
                out=bias_words[:, :, c0 : c0 + 4], in_=acc[:].rearrange("p (c n) -> p n c", c=4)
            )

        table_shape = [P, TOK_TILES, HALF]
        ang = const.tile(table_shape, F32, name="ang")
        nc.vector.tensor_copy(out=ang[:, :, 0:1], in_=pos[:].unsqueeze(2))
        for w in (1, 2, 4, 8):
            nc.vector.tensor_scalar(
                out=ang[:, :, w : 2 * w], in0=ang[:, :, 0:w],
                scalar1=10000.0 ** (-w / 16.0), scalar2=None, op0=ALU.mult,
            )
        turns_i = const.tile(table_shape, I32, name="turns_i")
        nc.vector.tensor_scalar(
            out=turns_i[:], in0=ang[:], scalar1=1.0 / TWO_PI, scalar2=0.25,
            op0=ALU.mult, op1=ALU.add,
        )
        turns = const.tile(table_shape, F32, name="turns")
        nc.vector.tensor_copy(out=turns[:], in_=turns_i[:])
        red = const.tile(table_shape, F32, name="red")
        nc.vector.scalar_tensor_tensor(
            out=red[:], in0=turns[:], scalar=-C1, in1=ang[:], op0=ALU.mult, op1=ALU.add
        )
        for cc in (C2, C3):
            nc.vector.scalar_tensor_tensor(
                out=red[:], in0=turns[:], scalar=-cc, in1=red[:], op0=ALU.mult, op1=ALU.add
            )
        sin_half = const.tile(table_shape, F32, name="sin_half")
        sin_quarter = const.tile(table_shape, F32, name="sin_quarter")
        nc.scalar.activation(out=sin_half[:], in_=red[:], func=ACT.Sin, scale=0.5)
        nc.scalar.activation(out=sin_quarter[:], in_=red[:], func=ACT.Sin, scale=0.25)

        nc.gpsimd.memset(w_planes[2][:].bitcast(F32), 0.0)
        load_plane(w_planes[2], w_scales[:, :, 3072:6144])

        cos_t = const.tile(table_shape, F32, name="cos_t")
        sin_t = const.tile(table_shape, F32, name="sin_t")
        cos_half = const.tile(table_shape, F32, name="cos_half")

        def finish_tables():
            nc.vector.tensor_tensor(out=cos_t[:], in0=sin_half[:], in1=sin_half[:], op=ALU.mult)
            nc.vector.tensor_scalar(
                out=cos_t[:], in0=cos_t[:], scalar1=-2.0, scalar2=1.0, op0=ALU.mult, op1=ALU.add
            )
            nc.vector.tensor_tensor(
                out=cos_half[:], in0=sin_quarter[:], in1=sin_quarter[:], op=ALU.mult
            )
            nc.vector.tensor_scalar(
                out=cos_half[:], in0=cos_half[:], scalar1=-2.0, scalar2=1.0, op0=ALU.mult, op1=ALU.add
            )
            nc.vector.scalar_tensor_tensor(
                out=sin_t[:], in0=sin_half[:], scalar=2.0, in1=cos_half[:], op0=ALU.mult, op1=ALU.mult
            )

        def w_operand(col, n, g):
            if col < BANK:
                if g == 0:
                    codes = w_first[:, 2 * col : 2 * (col + n)]
                else:
                    codes = w_first_rest[:, g - 1, 2 * col : 2 * (col + n)]
            else:
                i = [k for k, (a, b) in enumerate(CODE_CHUNKS) if a <= col < b][0]
                off = col - CODE_CHUNKS[i][0]
                codes = w_chunks[i][:, g, 2 * off : 2 * (off + n)]
            i = [k for k, (a, b) in enumerate(PLANE_CHUNKS) if a <= col < b][0]
            off = col - PLANE_CHUNKS[i][0]
            return codes.bitcast(FP4X4), w_planes[i][:, g, off : off + n]

        def one_pass(out, col, n, m, g):
            codes, plane = w_operand(col, n, g)
            if g == 0:
                tokens = hid_first[:, 2 * P * m : 2 * P * (m + 1)]
            else:
                tokens = hid_rest[:, g - 1, 2 * P * m : 2 * P * (m + 1)]
            nc.tensor.matmul_mx(
                out=out,
                lhsT=tokens.bitcast(FP4X4),
                lhsT_scale=hid_plane[:, g, P * m : P * (m + 1)],
                rhs=codes,
                rhs_scale=plane,
                start=(g == 0),
                stop=(g == PASSES - 1),
            )

        stages = {}
        for gi, (h0, nh) in enumerate(GROUPS):
            for m in range(TOK_TILES):
                st = const.tile([P, 3, nh, HEAD_DIM], F32, name="stage_%d_%d" % (gi, m), align_bytes=256)
                stages[(gi, m)] = st

        rotary = []
        for m in range(TOK_TILES):
            rot = const.tile([P, ROT, GROUPS[1][1], 2], F32, name="rotary_%d" % m)
            rotary.append(rot)

        def group_of(head):
            return [gi for gi, (h0, nh) in enumerate(GROUPS) if h0 <= head < h0 + nh][0]

        def evacuate(acc, c, m):
            blocks = [divmod(4 * c + i, 3) for i in range(4)]
            start = 0
            for i in range(1, 5):
                if i == 4 or blocks[i][0] != blocks[start][0]:
                    head, kind = blocks[start]
                    n = i - start
                    gi = group_of(head)
                    nc.vector.tensor_tensor(
                        out=stages[(gi, m)][:, kind : kind + n, head - GROUPS[gi][0], :],
                        in0=acc[:, P * start : P * i].rearrange("p (b d) -> p b d", d=HEAD_DIM),
                        in1=bias_heads[:, head, kind : kind + n, :],
                        op=ALU.add,
                    )
                    start = i

        def bank_job(c, m):
            acc = psum.tile([P, BANK], F32, name="acc", tag="acc")
            for g in range(PASSES):
                one_pass(acc[:], c * BANK, BANK, m, g)
            evacuate(acc, c, m)

        def qk_bank_job(head, m):
            acc = psum.tile([P, BANK], F32, name="acc", tag="acc")
            for i in range(2):
                for g in range(PASSES):
                    one_pass(acc[:, 256 * i : 256 * (i + 1)], (head + i) * HEAD_COLS, 256, m, g)
            gi = group_of(head)
            hl = head - GROUPS[gi][0]
            sums = acc[:].rearrange("p (h k d) -> p h k d", k=2, d=HEAD_DIM)
            nc.vector.tensor_tensor(
                out=rotary[m][:, :, hl : hl + 2, :],
                in0=sums[:, :, :, 0:ROT].rearrange("p h k d -> p d h k"),
                in1=bias_heads[:, head : head + 2, 0:2, 0:ROT].rearrange("p h k d -> p d h k"),
                op=ALU.add,
            )
            nc.vector.tensor_tensor(
                out=stages[(gi, m)][:, 0:2, hl : hl + 2, ROT:HEAD_DIM].rearrange("p k h d -> p h k d"),
                in0=sums[:, :, :, ROT:HEAD_DIM],
                in1=bias_heads[:, head : head + 2, 0:2, ROT:HEAD_DIM],
                op=ALU.add,
            )

        def v_bank_job(head, m):
            acc = psum.tile([P, BANK], F32, name="acc", tag="acc")
            for i in range(4):
                for g in range(PASSES):
                    one_pass(
                        acc[:, P * i : P * (i + 1)], (head + i) * HEAD_COLS + 2 * HEAD_DIM, P, m, g
                    )
            gi = group_of(head)
            hl = head - GROUPS[gi][0]
            nc.vector.tensor_tensor(
                out=stages[(gi, m)][:, 2, hl : hl + 4, :],
                in0=acc[:].rearrange("p (h d) -> p h d", d=HEAD_DIM),
                in1=bias_heads[:, head : head + 4, 2, :],
                op=ALU.add,
            )

        def store(gi, m, kind, hl=0, n=None):
            h0, nh = GROUPS[gi]
            n = nh if n is None else n
            nc.sync.dma_start(
                out=outs[kind][P * m : P * (m + 1), 0, h0 + hl : h0 + hl + n, :],
                in_=stages[(gi, m)][:, kind, hl : hl + n, :],
            )

        def rope_products(gi, m):
            st = stages[(gi, m)]
            nh = GROUPS[gi][1]
            by_cos = tmp_pool.tile([P, HALF, 2, nh, 2], F32, name="by_cos", tag="by_cos%d" % nh)
            by_sin = tmp_pool.tile([P, HALF, 2, nh, 2], F32, name="by_sin", tag="by_sin%d" % nh)
            for j in range(HALF):
                src = st[:, 0:2, :, j : j + HALF + 1 : HALF] if gi == 0 else rotary[m][:, j : j + HALF + 1 : HALF, :, :]
                nc.scalar.activation(
                    out=by_cos[:, j, :, :, :], in_=src, func=ACT.Copy, scale=cos_t[:, m, j : j + 1]
                )
                nc.scalar.activation(
                    out=by_sin[:, j, :, :, :], in_=src, func=ACT.Copy, scale=sin_t[:, m, j : j + 1]
                )
            return by_cos, by_sin

        def rope_sums(gi, m, engine, by_cos, by_sin):
            st = stages[(gi, m)]

            def part(products, kind, t):
                view = products[:, :, kind, :, t] if gi == 0 else products[:, :, t, :, kind]
                return view.rearrange("p j h -> p h j")

            for kind in range(2):
                engine.tensor_tensor(
                    out=st[:, kind, :, 0:HALF],
                    in0=part(by_cos, kind, 0), in1=part(by_sin, kind, 1), op=ALU.subtract,
                )
                engine.tensor_tensor(
                    out=st[:, kind, :, HALF : 2 * HALF],
                    in0=part(by_cos, kind, 1), in1=part(by_sin, kind, 0), op=ALU.add,
                )

        waiting = []

        def flush_waiting():
            for gi, m in waiting:
                store(gi, m, 0)
                store(gi, m, 1)
            waiting.clear()

        accs = []
        for m in range(TOK_TILES):
            acc = psum.tile([P, BANK], F32, name="acc", tag="acc")
            accs.append(acc)
        for g in range(PASSES):
            for m in range(TOK_TILES):
                one_pass(accs[m][:], 0, BANK, m, g)
        for m in range(TOK_TILES):
            evacuate(accs[m], 0, m)
        finish_tables()

        for m in range(TOK_TILES):
            bank_job(1, m)

        for m in range(TOK_TILES):
            for c in (2, 3, 4, 5):
                bank_job(c, m)
            store(0, m, 2)
            flush_waiting()
            by_cos, by_sin = rope_products(0, m)
            rope_sums(0, m, nc.gpsimd, by_cos, by_sin)
            waiting.append((0, m))

        def v_tile(m):
            for head in (8, 12):
                v_bank_job(head, m)
                store(1, m, 2, head - 8, 4)

        for m in range(TOK_TILES):
            if m == TOK_TILES - 1:
                for early in range(V_EARLY):
                    v_tile(early)
            for head in (8, 10, 12, 14):
                qk_bank_job(head, m)
            flush_waiting()
            by_cos, by_sin = rope_products(1, m)
            if m < TOK_TILES - 1:
                rope_sums(1, m, nc.gpsimd, by_cos, by_sin)
                waiting.append((1, m))
        late = [(m, head) for m in range(V_EARLY, TOK_TILES) for head in (8, 12)]
        for i, (m, head) in enumerate(late):
            if i == SUMS_BEHIND:
                rope_sums(1, 3, nc.vector, by_cos, by_sin)
                store(1, 3, 0)
                store(1, 3, 1)
            v_bank_job(head, m)
            store(1, m, 2, head - 8, 4)
